import numpy as np
import ml_dtypes


def mxq(x, axis, fmt="e4m3"):
    dtype, down = {"e4m3": (ml_dtypes.float8_e4m3fn, 7), "e5m2": (ml_dtypes.float8_e5m2, 14)}[fmt]
    v = np.moveaxis(np.asarray(x, np.float32).astype(ml_dtypes.bfloat16).astype(np.float64), axis, -1)
    blocks = v.reshape(v.shape[:-1] + (-1, 32))
    amax = np.abs(blocks).max(-1, keepdims=True)
    byte = np.maximum(np.where(amax > 0, np.frexp(amax)[1] - 1 + 127, 0) - down, 1)
    scale = np.exp2(byte - 127.0)
    codes = (blocks / scale).astype(np.float32).astype(dtype).astype(np.float64)
    return np.moveaxis((codes * scale).reshape(v.shape), -1, axis)


WIDE = False


def mx_kscale(k):
    if not WIDE:
        return np.ones(k)
    levels = np.array([10, -10, 5, -5, 0])
    a = np.random.permutation(np.resize(levels, k // 512 * 4)).reshape(k // 512, 4)
    idx = np.arange(k)
    return np.exp2(a[idx // 512, idx % 128 // 32])


BF16 = ml_dtypes.bfloat16


def bf(x):
    return np.asarray(x, np.float32).astype(BF16)


def f64(x):
    return np.asarray(x).astype(np.float64)


B, N = 16384, 256
SLOPE = 0.01


def setup_inputs():
    s = mx_kscale(B)
    level = np.random.standard_normal(N) * 2.5 - 1.5
    return {"potential": bf((np.random.standard_normal((B, N)) * 2.2 + level) * s[:, None]),
            "contribution": bf(np.random.random(B) / (s * s))}


def reference(potential, contribution):
    p = f64(potential)
    activation = np.where(p >= 0, p, SLOPE * p)
    weighted = activation * f64(contribution)[:, None]
    return (mxq(weighted, 0, "e4m3").T @ mxq(activation, 0, "e4m3")) / B

@@ -1,0 +1,190 @@
+from contextlib import ExitStack
+
+import concourse.mybir as mybir
+
+FLOPS = 2 * 16384 * 256 * 256
+
+BF16 = mybir.dt.bfloat16
+F32 = mybir.dt.float32
+U32 = mybir.dt.uint32
+U8 = mybir.dt.uint8
+FP8X4 = mybir.dt.float8_e4m3fn_x4
+ALU = mybir.AluOpType
+ACTF = mybir.ActivationFunctionType
+
+P = 128
+PACK = 4
+N = 256
+B = 16384
+K_PASS = P * PACK
+PASSES = B // K_PASS
+SLOPE = 0.01
+SIZES = [1,1,2,2,2,2,2,2,2,2,2,2,2,2,2,2,1,1]
+MANUAL = True
+V_SCALE = {}
+V_WPERM = []
+S_APERM = []
+BUFS = 3
+
+
+def tile_mnelayer_pb_t_kernel(tc, potential, contribution, out):
+    nc = tc.nc
+    assert sum(SIZES) == PASSES
+    n_ch = len(SIZES)
+    starts = [sum(SIZES[:i]) for i in range(n_ch)]
+    with ExitStack() as ctx:
+        keep = ctx.enter_context(tc.tile_pool(name="keep", bufs=1))
+        work = ctx.enter_context(tc.tile_pool(name="work", bufs=BUFS))
+        psum = ctx.enter_context(tc.psum_pool(name="psum", bufs=1))
+        if MANUAL:
+            ctx.enter_context(tc.manual_schedule())
+
+        pot = potential.rearrange("(g p j) n -> p g (j n)", p=P, j=PACK)
+        con = contribution.rearrange("(g p j) -> p g j", p=P, j=PACK)
+
+        c_bf = keep.tile([P, PASSES, PACK], BF16)
+        c32 = keep.tile([P, PASSES * PACK], F32)
+        nc.scalar.dma_start(out=c_bf[:], in_=con)
+
+        raws = []
+        for i in range(n_ch):
+            raw = keep.tile([P, SIZES[i], PACK * N], BF16, name="raw%d" % i)
+            nc.sync.dma_start(out=raw[:], in_=pot[:, starts[i] : starts[i] + SIZES[i], :])
+            raws.append(raw)
+
+        nc.scalar.activation(
+            out=c32[:], in_=c_bf[:].rearrange("p g j -> p (g j)"), func=ACTF.Copy
+        )
+
+        acc0 = psum.tile([P, N], F32)
+        acc1 = psum.tile([P, N], F32)
+        accs = [acc0, acc1]
+        st = {}
+
+        def regroup(eng_copy, dst, src):
+            eng_copy(
+                out=dst.rearrange("p (c i) t -> p c t i", i=4),
+                in_=src.rearrange("p t (c i) -> p c t i", i=4),
+            )
+
+        def d1(i):
+            sz = SIZES[i]
+            leak = work.tile([P, sz, PACK, N], F32, name="leak", tag="leak%d" % sz)
+            flat = raws[i][:].rearrange("p g f -> p (g f)")
+            nc.vector.scalar_tensor_tensor(
+                out=leak[:].rearrange("p g j n -> p (g j n)"),
+                in0=flat,
+                scalar=SLOPE,
+                in1=flat,
+                op0=ALU.mult,
+                op1=ALU.max,
+            )
+            st[("leak", i)] = leak
+
+        def a_perm(i):
+            sz = SIZES[i]
+            leak = st[("leak", i)]
+            a_grp = work.tile([P, sz, N, PACK], BF16, name="a_grp", tag="a_grp%d" % sz, align_bytes=64)
+            for g in range(sz):
+                if i in S_APERM:
+                    regroup(nc.scalar.copy, a_grp[:, g], leak[:, g])
+                else:
+                    regroup(nc.vector.tensor_copy, a_grp[:, g], leak[:, g])
+            st[("a_grp", i)] = a_grp
+
+        def w_scale(i, who):
+            sz = SIZES[i]
+            leak = st[("leak", i)]
+            if ("w_nat", i) not in st:
+                w_nat_new = work.tile([P, sz, PACK, N], BF16, name="w_nat", tag="w_nat%d" % sz)
+                st[("w_nat", i)] = w_nat_new
+            w_nat = st[("w_nat", i)]
+            n_v = V_SCALE.get(str(i), 0)
+            for g in range(sz):
+                for j in range(PACK):
+                    col = (starts[i] + g) * PACK + j
+                    on_v = (g * PACK + j) >= sz * PACK - n_v
+                    if on_v and who == "V":
+                        nc.vector.tensor_scalar(
+                            out=w_nat[:, g, j, :],
+                            in0=leak[:, g, j, :],
+                            scalar1=c32[:, col : col + 1],
+                            scalar2=None,
+                            op0=ALU.mult,
+                        )
+                    if (not on_v) and who == "S":
+                        nc.scalar.activation(
+                            out=w_nat[:, g, j, :],
+                            in_=leak[:, g, j, :],
+                            func=ACTF.Copy,
+                            scale=c32[:, col : col + 1],
+                        )
+
+        def w_perm(i, who):
+            sz = SIZES[i]
+            w_nat = st[("w_nat", i)]
+            on_v = i in V_WPERM
+            if on_v != (who == "V"):
+                return
+            w_grp = work.tile([P, sz, N, PACK], BF16, name="w_grp", tag="w_grp%d" % sz, align_bytes=64)
+            for g in range(sz):
+                if on_v:
+                    regroup(nc.vector.tensor_copy, w_grp[:, g], w_nat[:, g])
+                else:
+                    regroup(nc.scalar.copy, w_grp[:, g], w_nat[:, g])
+            st[("w_grp", i)] = w_grp
+
+        def quant(i, what):
+            sz = SIZES[i]
+            grp = st[(what + "_grp", i)]
+            codes = work.tile([P, sz * N], U32, name=what + "_codes", tag="%s_codes%d" % (what, sz), align_bytes=64)
+            scales = work.tile([P, sz * N], U8, name=what + "_scales", tag="%s_scales%d" % (what, sz), align_bytes=64)
+            nc.vector.quantize_mx(
+                out=codes[:].bitcast(FP8X4),
+                scales=scales[:],
+                in_=grp[:].rearrange("p g n t -> p (g n t)"),
+            )
+            st[(what + "_q", i)] = (codes, scales)
+
+        def mm(i):
+            sz = SIZES[i]
+            a_codes, a_scales = st[("a_q", i)]
+            w_codes, w_scales = st[("w_q", i)]
+            for g in range(sz):
+                first = i == 0 and g == 0
+                last = i == n_ch - 1 and g == sz - 1
+                for m in range(2):
+                    lo = g * N + m * P
+                    nc.tensor.matmul_mx(
+                        out=accs[m][:],
+                        lhsT=w_codes[:, lo : lo + P].bitcast(FP8X4),
+                        lhsT_scale=w_scales[:, lo : lo + P],
+                        rhs=a_codes[:, g * N : (g + 1) * N].bitcast(FP8X4),
+                        rhs_scale=a_scales[:, g * N : (g + 1) * N],
+                        start=first,
+                        stop=last,
+                    )
+
+        for t in range(n_ch + 1):
+            if t < n_ch:
+                d1(t)
+                w_scale(t, "S")
+            if t >= 1:
+                quant(t - 1, "a")
+            if t < n_ch:
+                w_scale(t, "V")
+                a_perm(t)
+                w_perm(t, "S")
+                w_perm(t, "V")
+            if t >= 1:
+                quant(t - 1, "w")
+                mm(t - 1)
+
+        res0 = keep.tile([P, N], F32)
+        res1 = keep.tile([P, N], F32)
+        nc.vector.tensor_scalar(
+            out=res0[:], in0=acc0[:], scalar1=1.0 / B, scalar2=None, op0=ALU.mult
+        )
+        nc.scalar.activation(out=res1[:], in_=acc1[:], func=ACTF.Copy, scale=1.0 / B)
+        nc.sync.dma_start(out=out[0:P, :], in_=res0[:])
+        nc.scalar.dma_start(out=out[P : 2 * P, :], in_=res1[:])

@@ -21,10 +21,12 @@ PASSES = B // K_PASS
 SLOPE = 0.01
 SIZES = [1,1,2,2,2,2,2,2,2,2,2,2,2,2,2,2,1,1]
 MANUAL = True
-V_SCALE = {}
-V_WPERM = []
-S_APERM = []
-BUFS = 3
+V_SCALE = {"17":2}
+V_WPERM = {"17":128}
+S_APERM = {}
+BUFS = 4
+LAG1 = 1
+LAG2 = 2
 
 
 def tile_mnelayer_pb_t_kernel(tc, potential, contribution, out):
@@ -61,10 +63,10 @@ def tile_mnelayer_pb_t_kernel(tc, potential, contribution, out):
         accs = [acc0, acc1]
         st = {}
 
-        def regroup(eng_copy, dst, src):
+        def regroup(eng_copy, dst, src, lo, hi):
             eng_copy(
-                out=dst.rearrange("p (c i) t -> p c t i", i=4),
-                in_=src.rearrange("p t (c i) -> p c t i", i=4),
+                out=dst[:, lo:hi, :].rearrange("p (c i) t -> p c t i", i=4),
+                in_=src[:, :, lo:hi].rearrange("p t (c i) -> p c t i", i=4),
             )
 
         def d1(i):
@@ -80,24 +82,25 @@ def tile_mnelayer_pb_t_kernel(tc, potential, contribution, out):
                 op1=ALU.max,
             )
             st[("leak", i)] = leak
+            st[("a_grp", i)] = work.tile([P, sz, N, PACK], BF16, name="a_grp", tag="a_grp%d" % sz, align_bytes=64)
+            st[("w_nat", i)] = work.tile([P, sz, PACK, N], BF16, name="w_nat", tag="w_nat%d" % sz)
+            st[("w_grp", i)] = work.tile([P, sz, N, PACK], BF16, name="w_grp", tag="w_grp%d" % sz, align_bytes=64)
 
-        def a_perm(i):
+        def perm(i, what, who):
             sz = SIZES[i]
-            leak = st[("leak", i)]
-            a_grp = work.tile([P, sz, N, PACK], BF16, name="a_grp", tag="a_grp%d" % sz, align_bytes=64)
+            if what == "a":
+                src, dst, cut = st[("leak", i)], st[("a_grp", i)], S_APERM.get(str(i), 0)
+            else:
+                src, dst, cut = st[("w_nat", i)], st[("w_grp", i)], N - V_WPERM.get(str(i), 0)
             for g in range(sz):
-                if i in S_APERM:
-                    regroup(nc.scalar.copy, a_grp[:, g], leak[:, g])
-                else:
-                    regroup(nc.vector.tensor_copy, a_grp[:, g], leak[:, g])
-            st[("a_grp", i)] = a_grp
+                if who == "S" and cut > 0:
+                    regroup(nc.scalar.copy, dst[:, g], src[:, g], 0, cut)
+                if who == "V" and cut < N:
+                    regroup(nc.vector.tensor_copy, dst[:, g], src[:, g], cut, N)
 
         def w_scale(i, who):
             sz = SIZES[i]
             leak = st[("leak", i)]
-            if ("w_nat", i) not in st:
-                w_nat_new = work.tile([P, sz, PACK, N], BF16, name="w_nat", tag="w_nat%d" % sz)
-                st[("w_nat", i)] = w_nat_new
             w_nat = st[("w_nat", i)]
             n_v = V_SCALE.get(str(i), 0)
             for g in range(sz):
@@ -119,20 +122,6 @@ def tile_mnelayer_pb_t_kernel(tc, potential, contribution, out):
                             func=ACTF.Copy,
                             scale=c32[:, col : col + 1],
                         )
-
-        def w_perm(i, who):
-            sz = SIZES[i]
-            w_nat = st[("w_nat", i)]
-            on_v = i in V_WPERM
-            if on_v != (who == "V"):
-                return
-            w_grp = work.tile([P, sz, N, PACK], BF16, name="w_grp", tag="w_grp%d" % sz, align_bytes=64)
-            for g in range(sz):
-                if on_v:
-                    regroup(nc.vector.tensor_copy, w_grp[:, g], w_nat[:, g])
-                else:
-                    regroup(nc.scalar.copy, w_grp[:, g], w_nat[:, g])
-            st[("w_grp", i)] = w_grp
 
         def quant(i, what):
             sz = SIZES[i]
@@ -165,20 +154,24 @@ def tile_mnelayer_pb_t_kernel(tc, potential, contribution, out):
                         stop=last,
                     )
 
-        for t in range(n_ch + 1):
+        for t in range(n_ch + LAG2):
+            u = t - LAG1
+            v = t - LAG2
             if t < n_ch:
                 d1(t)
-                w_scale(t, "S")
-            if t >= 1:
-                quant(t - 1, "a")
-            if t < n_ch:
-                w_scale(t, "V")
-                a_perm(t)
-                w_perm(t, "S")
-                w_perm(t, "V")
-            if t >= 1:
-                quant(t - 1, "w")
-                mm(t - 1)
+            if 0 <= u < n_ch:
+                w_scale(u, "S")
+                w_scale(u, "V")
+            if 0 <= v < n_ch:
+                quant(v, "a")
+            if 0 <= u < n_ch:
+                perm(u, "a", "V")
+                perm(u, "w", "S")
+                perm(u, "a", "S")
+                perm(u, "w", "V")
+            if 0 <= v < n_ch:
+                quant(v, "w")
+                mm(v)
 
         res0 = keep.tile([P, N], F32)
         res1 = keep.tile([P, N], F32)

@@ -25,6 +25,7 @@ V_SCALE = {"17":2}
 V_WPERM = {"17":128}
 S_APERM = {}
 BUFS = 4
+C_CUTS = [0,2,8,32]
 LAG1 = 1
 LAG2 = 2
 
@@ -44,9 +45,25 @@ def tile_mnelayer_pb_t_kernel(tc, potential, contribution, out):
         pot = potential.rearrange("(g p j) n -> p g (j n)", p=P, j=PACK)
         con = contribution.rearrange("(g p j) -> p g j", p=P, j=PACK)
 
-        c_bf = keep.tile([P, PASSES, PACK], BF16)
         c32 = keep.tile([P, PASSES * PACK], F32)
-        nc.scalar.dma_start(out=c_bf[:], in_=con)
+        c_parts = []
+        for k in range(len(C_CUTS) - 1):
+            lo, hi = C_CUTS[k], C_CUTS[k + 1]
+            c_bf = keep.tile([P, hi - lo, PACK], BF16, name="c_bf%d" % k)
+            nc.scalar.dma_start(out=c_bf[:], in_=con[:, lo:hi, :])
+            c_parts.append(c_bf)
+        cast_done = []
+
+        def cast_c(upto):
+            for k in range(len(C_CUTS) - 1):
+                lo, hi = C_CUTS[k], C_CUTS[k + 1]
+                if k not in cast_done and lo < upto:
+                    nc.scalar.activation(
+                        out=c32[:, lo * PACK : hi * PACK],
+                        in_=c_parts[k][:].rearrange("p g j -> p (g j)"),
+                        func=ACTF.Copy,
+                    )
+                    cast_done.append(k)
 
         raws = []
         for i in range(n_ch):
@@ -54,9 +71,6 @@ def tile_mnelayer_pb_t_kernel(tc, potential, contribution, out):
             nc.sync.dma_start(out=raw[:], in_=pot[:, starts[i] : starts[i] + SIZES[i], :])
             raws.append(raw)
 
-        nc.scalar.activation(
-            out=c32[:], in_=c_bf[:].rearrange("p g j -> p (g j)"), func=ACTF.Copy
-        )
 
         acc0 = psum.tile([P, N], F32)
         acc1 = psum.tile([P, N], F32)
@@ -160,6 +174,7 @@ def tile_mnelayer_pb_t_kernel(tc, potential, contribution, out):
             if t < n_ch:
                 d1(t)
             if 0 <= u < n_ch:
+                cast_c(starts[u] + SIZES[u])
                 w_scale(u, "S")
                 w_scale(u, "V")
             if 0 <= v < n_ch:

@@ -21,11 +21,12 @@ PASSES = B // K_PASS
 SLOPE = 0.01
 SIZES = [1,1,2,2,2,2,2,2,2,2,2,2,2,2,2,2,1,1]
 MANUAL = True
-V_SCALE = {"17":2}
+V_SCALE = {"3":1,"5":1,"7":1,"9":1,"11":1,"13":1,"15":1,"17":2}
 V_WPERM = {"17":128}
 S_APERM = {}
 BUFS = 4
 C_CUTS = [0,2,8,32]
+D1_SPLIT = {"0":2}
 LAG1 = 1
 LAG2 = 2
 
@@ -87,14 +88,18 @@ def tile_mnelayer_pb_t_kernel(tc, potential, contribution, out):
             sz = SIZES[i]
             leak = work.tile([P, sz, PACK, N], F32, name="leak", tag="leak%d" % sz)
             flat = raws[i][:].rearrange("p g f -> p (g f)")
-            nc.vector.scalar_tensor_tensor(
-                out=leak[:].rearrange("p g j n -> p (g j n)"),
-                in0=flat,
-                scalar=SLOPE,
-                in1=flat,
-                op0=ALU.mult,
-                op1=ALU.max,
-            )
+            flat_out = leak[:].rearrange("p g j n -> p (g j n)")
+            parts = D1_SPLIT.get(str(i), 1)
+            width = sz * PACK * N // parts
+            for h in range(parts):
+                nc.vector.scalar_tensor_tensor(
+                    out=flat_out[:, h * width : (h + 1) * width],
+                    in0=flat[:, h * width : (h + 1) * width],
+                    scalar=SLOPE,
+                    in1=flat[:, h * width : (h + 1) * width],
+                    op0=ALU.mult,
+                    op1=ALU.max,
+                )
             st[("leak", i)] = leak
             st[("a_grp", i)] = work.tile([P, sz, N, PACK], BF16, name="a_grp", tag="a_grp%d" % sz, align_bytes=64)
             st[("w_nat", i)] = work.tile([P, sz, PACK, N], BF16, name="w_nat", tag="w_nat%d" % sz)
@@ -171,12 +176,13 @@ def tile_mnelayer_pb_t_kernel(tc, potential, contribution, out):
         for t in range(n_ch + LAG2):
             u = t - LAG1
             v = t - LAG2
+            if 0 <= u < n_ch:
+                cast_c(starts[u] + SIZES[u])
+                w_scale(u, "V")
             if t < n_ch:
                 d1(t)
             if 0 <= u < n_ch:
-                cast_c(starts[u] + SIZES[u])
                 w_scale(u, "S")
-                w_scale(u, "V")
             if 0 <= v < n_ch:
                 quant(v, "a")
             if 0 <= u < n_ch:

@@ -21,7 +21,7 @@ PASSES = B // K_PASS
 SLOPE = 0.01
 SIZES = [1,1,2,2,2,2,2,2,2,2,2,2,2,2,2,2,1,1]
 MANUAL = True
-V_SCALE = {"3":1,"5":1,"7":1,"9":1,"11":1,"13":1,"15":1,"17":2}
+V_SCALE = {"4":1,"8":1,"12":1,"15":1,"17":2}
 V_WPERM = {"17":128}
 S_APERM = {}
 BUFS = 4
@@ -201,4 +201,4 @@ def tile_mnelayer_pb_t_kernel(tc, potential, contribution, out):
         )
         nc.scalar.activation(out=res1[:], in_=acc1[:], func=ACTF.Copy, scale=1.0 / B)
         nc.sync.dma_start(out=out[0:P, :], in_=res0[:])
-        nc.scalar.dma_start(out=out[P : 2 * P, :], in_=res1[:])
+        nc.sync.dma_start(out=out[P : 2 * P, :], in_=res1[:])

@@ -1,6 +1,7 @@
 from contextlib import ExitStack
 
 import concourse.mybir as mybir
+from concourse.masks import make_identity
 
 FLOPS = 2 * 16384 * 256 * 256
 
@@ -25,7 +26,6 @@ V_SCALE = {"4":1,"8":1,"12":1,"15":1,"17":2}
 V_WPERM = {"17":128}
 S_APERM = {}
 BUFS = 4
-C_CUTS = [0,2,8,32]
 D1_SPLIT = {"0":2}
 LAG1 = 1
 LAG2 = 2
@@ -46,25 +46,21 @@ def tile_mnelayer_pb_t_kernel(tc, potential, contribution, out):
         pot = potential.rearrange("(g p j) n -> p g (j n)", p=P, j=PACK)
         con = contribution.rearrange("(g p j) -> p g j", p=P, j=PACK)
 
+        c_rows = keep.tile([P, K_PASS], BF16)
+        nc.vector.memset(c_rows[32:64, :], 0.0)
+        nc.vector.memset(c_rows[64:128, :], 0.0)
+        nc.scalar.dma_start(out=c_rows[0:PASSES, :], in_=contribution.rearrange("(g k) -> g k", k=K_PASS))
+        ident = keep.tile([P, P], BF16)
+        make_identity(nc, ident[:])
+        c_ps = psum.tile([P, PACK, P], BF16)
         c32 = keep.tile([P, PASSES * PACK], F32)
-        c_parts = []
-        for k in range(len(C_CUTS) - 1):
-            lo, hi = C_CUTS[k], C_CUTS[k + 1]
-            c_bf = keep.tile([P, hi - lo, PACK], BF16, name="c_bf%d" % k)
-            nc.scalar.dma_start(out=c_bf[:], in_=con[:, lo:hi, :])
-            c_parts.append(c_bf)
-        cast_done = []
-
-        def cast_c(upto):
-            for k in range(len(C_CUTS) - 1):
-                lo, hi = C_CUTS[k], C_CUTS[k + 1]
-                if k not in cast_done and lo < upto:
-                    nc.scalar.activation(
-                        out=c32[:, lo * PACK : hi * PACK],
-                        in_=c_parts[k][:].rearrange("p g j -> p (g j)"),
-                        func=ACTF.Copy,
-                    )
-                    cast_done.append(k)
+        for j in range(PACK):
+            nc.tensor.transpose(c_ps[:, j, :], c_rows[:, j : K_PASS : PACK], ident[:])
+        nc.scalar.activation(
+            out=c32[:].rearrange("p (g j) -> p g j", j=PACK),
+            in_=c_ps[:, :, 0:PASSES].rearrange("p j g -> p g j"),
+            func=ACTF.Copy,
+        )
 
         raws = []
         for i in range(n_ch):
@@ -177,7 +173,6 @@ def tile_mnelayer_pb_t_kernel(tc, potential, contribution, out):
             u = t - LAG1
             v = t - LAG2
             if 0 <= u < n_ch:
-                cast_c(starts[u] + SIZES[u])
                 w_scale(u, "V")
             if t < n_ch:
                 d1(t)

@@ -20,31 +20,47 @@ B = 16384
 K_PASS = P * PACK
 PASSES = B // K_PASS
 SLOPE = 0.01
-SIZES = [1,1,2,2,2,2,2,2,2,2,2,2,2,2,2,2,1,1]
-MANUAL = True
-V_SCALE = {"4":1,"8":1,"12":1,"15":1,"17":2}
-V_WPERM = {"17":128}
-S_APERM = {}
+SIZES = [1, 1] + [2] * 14 + [1, 1]
 BUFS = 4
-D1_SPLIT = {"0":2}
 LAG1 = 1
 LAG2 = 2
+I_A = 4
+I_WS = 4
+I_WV = 4
+HEAD = 2
+
+
+def w_on_vector(p):
+    return p % 2 == 1 or p >= 30
+
+
+def a_on_vector(p):
+    return False
 
 
 def tile_mnelayer_pb_t_kernel(tc, potential, contribution, out):
     nc = tc.nc
-    assert sum(SIZES) == PASSES
+    assert sum(SIZES) == PASSES and SIZES[0] == 1
     n_ch = len(SIZES)
     starts = [sum(SIZES[:i]) for i in range(n_ch)]
     with ExitStack() as ctx:
         keep = ctx.enter_context(tc.tile_pool(name="keep", bufs=1))
         work = ctx.enter_context(tc.tile_pool(name="work", bufs=BUFS))
         psum = ctx.enter_context(tc.psum_pool(name="psum", bufs=1))
-        if MANUAL:
-            ctx.enter_context(tc.manual_schedule())
+        ctx.enter_context(tc.manual_schedule())
 
         pot = potential.rearrange("(g p j) n -> p g (j n)", p=P, j=PACK)
-        con = contribution.rearrange("(g p j) -> p g j", p=P, j=PACK)
+
+        raws = []
+        for i in range(n_ch):
+            raw = keep.tile([P, SIZES[i], PACK * N], BF16, name="raw%d" % i)
+            raws.append(raw)
+        head = PACK * N // HEAD
+        for h in range(HEAD):
+            cols = slice(h * head, (h + 1) * head)
+            nc.sync.dma_start(out=raws[0][:, :, cols], in_=pot[:, 0:1, cols])
+        for i in range(1, n_ch):
+            nc.sync.dma_start(out=raws[i][:], in_=pot[:, starts[i] : starts[i] + SIZES[i], :])
 
         c_rows = keep.tile([P, K_PASS], BF16)
         nc.vector.memset(c_rows[32:64, :], 0.0)
@@ -62,30 +78,23 @@ def tile_mnelayer_pb_t_kernel(tc, potential, contribution, out):
             func=ACTF.Copy,
         )
 
-        raws = []
-        for i in range(n_ch):
-            raw = keep.tile([P, SIZES[i], PACK * N], BF16, name="raw%d" % i)
-            nc.sync.dma_start(out=raw[:], in_=pot[:, starts[i] : starts[i] + SIZES[i], :])
-            raws.append(raw)
-
-
         acc0 = psum.tile([P, N], F32)
         acc1 = psum.tile([P, N], F32)
         accs = [acc0, acc1]
         st = {}
 
-        def regroup(eng_copy, dst, src, lo, hi):
-            eng_copy(
-                out=dst[:, lo:hi, :].rearrange("p (c i) t -> p c t i", i=4),
-                in_=src[:, :, lo:hi].rearrange("p t (c i) -> p c t i", i=4),
-            )
+        def grp(dst, i):
+            return dst.rearrange("p (c i) t -> p c t i", i=i)
 
-        def d1(i):
+        def nat(src, i):
+            return src.rearrange("p t (c i) -> p c t i", i=i)
+
+        def leaky(i):
             sz = SIZES[i]
             leak = work.tile([P, sz, PACK, N], F32, name="leak", tag="leak%d" % sz)
             flat = raws[i][:].rearrange("p g f -> p (g f)")
             flat_out = leak[:].rearrange("p g j n -> p (g j n)")
-            parts = D1_SPLIT.get(str(i), 1)
+            parts = HEAD if i == 0 else 1
             width = sz * PACK * N // parts
             for h in range(parts):
                 nc.vector.scalar_tensor_tensor(
@@ -101,52 +110,49 @@ def tile_mnelayer_pb_t_kernel(tc, potential, contribution, out):
             st[("w_nat", i)] = work.tile([P, sz, PACK, N], BF16, name="w_nat", tag="w_nat%d" % sz)
             st[("w_grp", i)] = work.tile([P, sz, N, PACK], BF16, name="w_grp", tag="w_grp%d" % sz, align_bytes=64)
 
-        def perm(i, what, who):
-            sz = SIZES[i]
-            if what == "a":
-                src, dst, cut = st[("leak", i)], st[("a_grp", i)], S_APERM.get(str(i), 0)
-            else:
-                src, dst, cut = st[("w_nat", i)], st[("w_grp", i)], N - V_WPERM.get(str(i), 0)
-            for g in range(sz):
-                if who == "S" and cut > 0:
-                    regroup(nc.scalar.copy, dst[:, g], src[:, g], 0, cut)
-                if who == "V" and cut < N:
-                    regroup(nc.vector.tensor_copy, dst[:, g], src[:, g], cut, N)
+        def a_copy(i, on_v):
+            for g in range(SIZES[i]):
+                if a_on_vector(starts[i] + g) == on_v:
+                    eng = nc.vector.tensor_copy if on_v else nc.scalar.copy
+                    eng(out=grp(st[("a_grp", i)][:, g], I_A), in_=nat(st[("leak", i)][:, g], I_A))
 
-        def w_scale(i, who):
-            sz = SIZES[i]
-            leak = st[("leak", i)]
-            w_nat = st[("w_nat", i)]
-            n_v = V_SCALE.get(str(i), 0)
-            for g in range(sz):
-                for j in range(PACK):
-                    col = (starts[i] + g) * PACK + j
-                    on_v = (g * PACK + j) >= sz * PACK - n_v
-                    if on_v and who == "V":
-                        nc.vector.tensor_scalar(
-                            out=w_nat[:, g, j, :],
-                            in0=leak[:, g, j, :],
-                            scalar1=c32[:, col : col + 1],
-                            scalar2=None,
-                            op0=ALU.mult,
-                        )
-                    if (not on_v) and who == "S":
+        def w_scale(i):
+            for g in range(SIZES[i]):
+                p = starts[i] + g
+                if not w_on_vector(p):
+                    for j in range(PACK):
                         nc.scalar.activation(
-                            out=w_nat[:, g, j, :],
-                            in_=leak[:, g, j, :],
+                            out=st[("w_nat", i)][:, g, j, :],
+                            in_=st[("leak", i)][:, g, j, :],
                             func=ACTF.Copy,
-                            scale=c32[:, col : col + 1],
+                            scale=c32[:, p * PACK + j : p * PACK + j + 1],
                         )
+
+        def w_copy(i):
+            for g in range(SIZES[i]):
+                if not w_on_vector(starts[i] + g):
+                    nc.scalar.copy(out=grp(st[("w_grp", i)][:, g], I_WS), in_=nat(st[("w_nat", i)][:, g], I_WS))
+
+        def w_fused(i):
+            for g in range(SIZES[i]):
+                p = starts[i] + g
+                if w_on_vector(p):
+                    nc.vector.tensor_tensor(
+                        out=grp(st[("w_grp", i)][:, g], I_WV),
+                        in0=nat(st[("leak", i)][:, g], I_WV),
+                        in1=nat(c32[:, p * PACK : (p + 1) * PACK].unsqueeze(2).to_broadcast([P, PACK, N]), I_WV),
+                        op=ALU.mult,
+                    )
 
         def quant(i, what):
             sz = SIZES[i]
-            grp = st[(what + "_grp", i)]
+            g4 = st[(what + "_grp", i)]
             codes = work.tile([P, sz * N], U32, name=what + "_codes", tag="%s_codes%d" % (what, sz), align_bytes=64)
             scales = work.tile([P, sz * N], U8, name=what + "_scales", tag="%s_scales%d" % (what, sz), align_bytes=64)
             nc.vector.quantize_mx(
                 out=codes[:].bitcast(FP8X4),
                 scales=scales[:],
-                in_=grp[:].rearrange("p g n t -> p (g n t)"),
+                in_=g4[:].rearrange("p g n t -> p (g n t)"),
             )
             st[(what + "_q", i)] = (codes, scales)
 
@@ -172,19 +178,17 @@ def tile_mnelayer_pb_t_kernel(tc, potential, contribution, out):
         for t in range(n_ch + LAG2):
             u = t - LAG1
             v = t - LAG2
-            if 0 <= u < n_ch:
-                w_scale(u, "V")
             if t < n_ch:
-                d1(t)
+                leaky(t)
             if 0 <= u < n_ch:
-                w_scale(u, "S")
+                w_scale(u)
             if 0 <= v < n_ch:
                 quant(v, "a")
             if 0 <= u < n_ch:
-                perm(u, "a", "V")
-                perm(u, "w", "S")
-                perm(u, "a", "S")
-                perm(u, "w", "V")
+                a_copy(u, True)
+                w_fused(u)
+                a_copy(u, False)
+                w_copy(u)
             if 0 <= v < n_ch:
                 quant(v, "w")
                 mm(v)

@@ -28,14 +28,15 @@ I_A = 4
 I_WS = 4
 I_WV = 4
 HEAD = 2
+GA = 96
 
 
 def w_on_vector(p):
-    return p % 2 == 1 or p >= 30
+    return p % 7 in (1, 3, 5) or p >= 30
 
 
-def a_on_vector(p):
-    return False
+def gp_neurons(p):
+    return GA if p % 2 == 0 and 2 <= p < 30 else 0
 
 
 def tile_mnelayer_pb_t_kernel(tc, potential, contribution, out):
@@ -110,11 +111,26 @@ def tile_mnelayer_pb_t_kernel(tc, potential, contribution, out):
             st[("w_nat", i)] = work.tile([P, sz, PACK, N], BF16, name="w_nat", tag="w_nat%d" % sz)
             st[("w_grp", i)] = work.tile([P, sz, N, PACK], BF16, name="w_grp", tag="w_grp%d" % sz, align_bytes=64)
 
-        def a_copy(i, on_v):
+        def a_copy(i):
             for g in range(SIZES[i]):
-                if a_on_vector(starts[i] + g) == on_v:
-                    eng = nc.vector.tensor_copy if on_v else nc.scalar.copy
-                    eng(out=grp(st[("a_grp", i)][:, g], I_A), in_=nat(st[("leak", i)][:, g], I_A))
+                lo = gp_neurons(starts[i] + g)
+                nc.scalar.copy(
+                    out=grp(st[("a_grp", i)][:, g, lo:N, :], I_A),
+                    in_=nat(st[("leak", i)][:, g, :, lo:N], I_A),
+                )
+
+        def a_gp(i):
+            for g in range(SIZES[i]):
+                hi = gp_neurons(starts[i] + g)
+                if hi > 0:
+                    nc.gpsimd.tensor_scalar(
+                        out=st[("a_grp", i)][:, g, 0:hi, :],
+                        in0=st[("leak", i)][:, g, :, 0:hi].rearrange("p t n -> p n t"),
+                        scalar1=1.0,
+                        scalar2=0.0,
+                        op0=ALU.mult,
+                        op1=ALU.add,
+                    )
 
         def w_scale(i):
             for g in range(SIZES[i]):
@@ -140,7 +156,7 @@ def tile_mnelayer_pb_t_kernel(tc, potential, contribution, out):
                     nc.vector.tensor_tensor(
                         out=grp(st[("w_grp", i)][:, g], I_WV),
                         in0=nat(st[("leak", i)][:, g], I_WV),
-                        in1=nat(c32[:, p * PACK : (p + 1) * PACK].unsqueeze(2).to_broadcast([P, PACK, N]), I_WV),
+                        in1=nat(c_ps[:, :, p : p + 1].to_broadcast([P, PACK, N]), I_WV),
                         op=ALU.mult,
                     )
 
@@ -180,16 +196,14 @@ def tile_mnelayer_pb_t_kernel(tc, potential, contribution, out):
             v = t - LAG2
             if t < n_ch:
                 leaky(t)
+                a_gp(t)
             if 0 <= u < n_ch:
                 w_scale(u)
-            if 0 <= v < n_ch:
-                quant(v, "a")
-            if 0 <= u < n_ch:
-                a_copy(u, True)
                 w_fused(u)
-                a_copy(u, False)
+                a_copy(u)
                 w_copy(u)
             if 0 <= v < n_ch:
+                quant(v, "a")
                 quant(v, "w")
                 mm(v)
 

@@ -27,16 +27,16 @@ LAG2 = 2
 I_A = 4
 I_WS = 4
 I_WV = 4
-HEAD = 2
-GA = 96
+HEAD = 4
+GA = 144
 
 
 def w_on_vector(p):
-    return p % 7 in (1, 3, 5) or p >= 30
+    return p >= 30 or (p % 2 == 1 and (p < 10 or p % 10 != 1))
 
 
 def gp_neurons(p):
-    return GA if p % 2 == 0 and 2 <= p < 30 else 0
+    return GA if p % 2 == 0 and 2 <= p < 30 and w_on_vector(p - 1) else 0
 
 
 def tile_mnelayer_pb_t_kernel(tc, potential, contribution, out):
@@ -95,7 +95,7 @@ def tile_mnelayer_pb_t_kernel(tc, potential, contribution, out):
             leak = work.tile([P, sz, PACK, N], F32, name="leak", tag="leak%d" % sz)
             flat = raws[i][:].rearrange("p g f -> p (g f)")
             flat_out = leak[:].rearrange("p g j n -> p (g j n)")
-            parts = HEAD if i == 0 else 1
+            parts = HEAD if i == 0 else sz
             width = sz * PACK * N // parts
             for h in range(parts):
                 nc.vector.scalar_tensor_tensor(

@@ -18,50 +18,62 @@ PACK = 4
 N = 256
 B = 16384
 K_PASS = P * PACK
+BANK = 512
 PASSES = B // K_PASS
 SLOPE = 0.01
-SIZES = [1, 1] + [2] * 14 + [1, 1]
-BUFS = 4
-LAG1 = 1
-LAG2 = 2
+SIZES = [1, 1, 2] + [4] * 6 + [2, 1, 1]
+STARTS = [sum(SIZES[:i]) for i in range(len(SIZES))]
+CHUNKS = len(SIZES)
+MAX = max(SIZES)
+BUFS = 3
 I_A = 4
 I_WS = 4
 I_WV = 4
-HEAD = 4
-GA = 144
+HEAD = 2
+GA = 160
 
 
-def w_on_vector(p):
-    return p >= 30 or (p % 2 == 1 and (p < 10 or p % 10 != 1))
+BIG = 4
+TWO_FUSED = (8,)
+LEAK_PARTS = [2, 1]
 
 
-def gp_neurons(p):
-    return GA if p % 2 == 0 and 2 <= p < 30 and w_on_vector(p - 1) else 0
+def w_engine(i, g):
+    if SIZES[i] == BIG:
+        if g == 0:
+            return "G"
+        return "V" if g == 3 or (g == 2 and i in TWO_FUSED) else "S"
+    p = STARTS[i] + g
+    return "V" if p in (1, 3) or p >= 29 else "S"
+
+
+def gp_passes(i):
+    return 1 if SIZES[i] == 2 else 0
 
 
 def tile_mnelayer_pb_t_kernel(tc, potential, contribution, out):
     nc = tc.nc
     assert sum(SIZES) == PASSES and SIZES[0] == 1
-    n_ch = len(SIZES)
-    starts = [sum(SIZES[:i]) for i in range(n_ch)]
     with ExitStack() as ctx:
         keep = ctx.enter_context(tc.tile_pool(name="keep", bufs=1))
         work = ctx.enter_context(tc.tile_pool(name="work", bufs=BUFS))
+        nats = ctx.enter_context(tc.tile_pool(name="nats", bufs=6))
+        copies = ctx.enter_context(tc.psum_pool(name="copies", bufs=2))
         psum = ctx.enter_context(tc.psum_pool(name="psum", bufs=1))
         ctx.enter_context(tc.manual_schedule())
 
         pot = potential.rearrange("(g p j) n -> p g (j n)", p=P, j=PACK)
 
         raws = []
-        for i in range(n_ch):
+        for i in range(CHUNKS):
             raw = keep.tile([P, SIZES[i], PACK * N], BF16, name="raw%d" % i)
             raws.append(raw)
         head = PACK * N // HEAD
         for h in range(HEAD):
             cols = slice(h * head, (h + 1) * head)
             nc.sync.dma_start(out=raws[0][:, :, cols], in_=pot[:, 0:1, cols])
-        for i in range(1, n_ch):
-            nc.sync.dma_start(out=raws[i][:], in_=pot[:, starts[i] : starts[i] + SIZES[i], :])
+        for i in range(1, CHUNKS):
+            nc.sync.dma_start(out=raws[i][:], in_=pot[:, STARTS[i] : STARTS[i] + SIZES[i], :])
 
         c_rows = keep.tile([P, K_PASS], BF16)
         nc.vector.memset(c_rows[32:64, :], 0.0)
@@ -92,67 +104,107 @@ def tile_mnelayer_pb_t_kernel(tc, potential, contribution, out):
 
         def leaky(i):
             sz = SIZES[i]
-            leak = work.tile([P, sz, PACK, N], F32, name="leak", tag="leak%d" % sz)
+            leak = work.tile([P, MAX, PACK, N], F32, name="leak", tag="leak")
             flat = raws[i][:].rearrange("p g f -> p (g f)")
-            flat_out = leak[:].rearrange("p g j n -> p (g j n)")
-            parts = HEAD if i == 0 else sz
-            width = sz * PACK * N // parts
-            for h in range(parts):
+            flat_out = leak[:, 0:sz].rearrange("p g j n -> p (g j n)")
+
+            def part(lo, hi, again):
                 nc.vector.scalar_tensor_tensor(
-                    out=flat_out[:, h * width : (h + 1) * width],
-                    in0=flat[:, h * width : (h + 1) * width],
+                    out=flat_out[:, lo:hi],
+                    in0=flat[:, lo:hi],
                     scalar=SLOPE,
-                    in1=flat[:, h * width : (h + 1) * width],
+                    in1=again,
                     op0=ALU.mult,
                     op1=ALU.max,
                 )
+
+            width = PACK * N
+            if i == 0:
+                for h in range(HEAD):
+                    part(h * head, (h + 1) * head, flat[:, h * head : (h + 1) * head])
+            elif sz < BIG:
+                part(0, sz * width, flat[:, 0 : sz * width])
+            else:
+                lo = 0
+                for w in LEAK_PARTS:
+                    part(lo * width, (lo + w) * width, flat[:, lo * width : (lo + w) * width])
+                    lo += w
+                for h in range(2):
+                    at = 3 * width + h * BANK
+                    part(at, at + BANK, st[("copy", i)][h][:])
             st[("leak", i)] = leak
-            st[("a_grp", i)] = work.tile([P, sz, N, PACK], BF16, name="a_grp", tag="a_grp%d" % sz, align_bytes=64)
-            st[("w_nat", i)] = work.tile([P, sz, PACK, N], BF16, name="w_nat", tag="w_nat%d" % sz)
-            st[("w_grp", i)] = work.tile([P, sz, N, PACK], BF16, name="w_grp", tag="w_grp%d" % sz, align_bytes=64)
+            st[("a_grp", i)] = work.tile([P, MAX, N, PACK], BF16, name="a_grp", tag="a_grp", align_bytes=64)
+            st[("w_grp", i)] = work.tile([P, MAX, N, PACK], BF16, name="w_grp", tag="w_grp", align_bytes=64)
+
+        def x_to_psum(i):
+            if SIZES[i] == BIG:
+                halves = []
+                for h in range(2):
+                    half = copies.tile([P, BANK], F32, name="half%d" % h, tag="half%d" % h)
+                    nc.tensor.matmul(
+                        out=half[:],
+                        lhsT=ident[:],
+                        rhs=raws[i][:, 3, h * BANK : (h + 1) * BANK],
+                        start=True,
+                        stop=True,
+                    )
+                    halves.append(half)
+                st[("copy", i)] = halves
+
+        def w_gp(i):
+            for g in range(SIZES[i]):
+                if w_engine(i, g) == "G":
+                    p = STARTS[i] + g
+                    nc.gpsimd.tensor_tensor(
+                        out=st[("w_grp", i)][:, g],
+                        in0=st[("leak", i)][:, g].rearrange("p t n -> p n t"),
+                        in1=c32[:, p * PACK : (p + 1) * PACK].unsqueeze(1).to_broadcast([P, N, PACK]),
+                        op=ALU.mult,
+                    )
+
+        def a_gp(i):
+            k = gp_passes(i)
+            if k > 0:
+                nc.gpsimd.tensor_scalar(
+                    out=st[("a_grp", i)][:, 0:k, 0:GA, :],
+                    in0=st[("leak", i)][:, 0:k, :, 0:GA].rearrange("p g t n -> p g n t"),
+                    scalar1=1.0,
+                    scalar2=0.0,
+                    op0=ALU.mult,
+                    op1=ALU.add,
+                )
 
         def a_copy(i):
             for g in range(SIZES[i]):
-                lo = gp_neurons(starts[i] + g)
+                lo = GA if g < gp_passes(i) else 0
                 nc.scalar.copy(
                     out=grp(st[("a_grp", i)][:, g, lo:N, :], I_A),
                     in_=nat(st[("leak", i)][:, g, :, lo:N], I_A),
                 )
 
-        def a_gp(i):
-            for g in range(SIZES[i]):
-                hi = gp_neurons(starts[i] + g)
-                if hi > 0:
-                    nc.gpsimd.tensor_scalar(
-                        out=st[("a_grp", i)][:, g, 0:hi, :],
-                        in0=st[("leak", i)][:, g, :, 0:hi].rearrange("p t n -> p n t"),
-                        scalar1=1.0,
-                        scalar2=0.0,
-                        op0=ALU.mult,
-                        op1=ALU.add,
-                    )
-
         def w_scale(i):
             for g in range(SIZES[i]):
-                p = starts[i] + g
-                if not w_on_vector(p):
+                if w_engine(i, g) == "S":
+                    p = STARTS[i] + g
+                    w_nat = nats.tile([P, PACK, N], BF16, name="w_nat", tag="w_nat")
                     for j in range(PACK):
                         nc.scalar.activation(
-                            out=st[("w_nat", i)][:, g, j, :],
+                            out=w_nat[:, j, :],
                             in_=st[("leak", i)][:, g, j, :],
                             func=ACTF.Copy,
                             scale=c32[:, p * PACK + j : p * PACK + j + 1],
                         )
+                    st[("w_nat", i, g)] = w_nat
 
         def w_copy(i):
             for g in range(SIZES[i]):
-                if not w_on_vector(starts[i] + g):
-                    nc.scalar.copy(out=grp(st[("w_grp", i)][:, g], I_WS), in_=nat(st[("w_nat", i)][:, g], I_WS))
+                if w_engine(i, g) == "S":
+                    nc.scalar.copy(out=grp(st[("w_grp", i)][:, g], I_WS), in_=nat(st[("w_nat", i, g)][:], I_WS))
 
         def w_fused(i):
             for g in range(SIZES[i]):
-                p = starts[i] + g
-                if w_on_vector(p):
+                if w_engine(i, g) == "V":
+                    p = STARTS[i] + g
                     nc.vector.tensor_tensor(
                         out=grp(st[("w_grp", i)][:, g], I_WV),
                         in0=nat(st[("leak", i)][:, g], I_WV),
@@ -163,22 +215,20 @@ def tile_mnelayer_pb_t_kernel(tc, potential, contribution, out):
         def quant(i, what):
             sz = SIZES[i]
             g4 = st[(what + "_grp", i)]
-            codes = work.tile([P, sz * N], U32, name=what + "_codes", tag="%s_codes%d" % (what, sz), align_bytes=64)
-            scales = work.tile([P, sz * N], U8, name=what + "_scales", tag="%s_scales%d" % (what, sz), align_bytes=64)
+            codes = work.tile([P, MAX * N], U32, name=what + "_codes", tag=what + "_codes", align_bytes=64)
+            scales = work.tile([P, MAX * N], U8, name=what + "_scales", tag=what + "_scales", align_bytes=64)
             nc.vector.quantize_mx(
-                out=codes[:].bitcast(FP8X4),
-                scales=scales[:],
-                in_=g4[:].rearrange("p g n t -> p (g n t)"),
+                out=codes[:, 0 : sz * N].bitcast(FP8X4),
+                scales=scales[:, 0 : sz * N],
+                in_=g4[:, 0:sz].rearrange("p g n t -> p (g n t)"),
             )
             st[(what + "_q", i)] = (codes, scales)
 
         def mm(i):
-            sz = SIZES[i]
             a_codes, a_scales = st[("a_q", i)]
             w_codes, w_scales = st[("w_q", i)]
-            for g in range(sz):
-                first = i == 0 and g == 0
-                last = i == n_ch - 1 and g == sz - 1
+            for g in range(SIZES[i]):
+                p = STARTS[i] + g
                 for m in range(2):
                     lo = g * N + m * P
                     nc.tensor.matmul_mx(
@@ -187,22 +237,24 @@ def tile_mnelayer_pb_t_kernel(tc, potential, contribution, out):
                         lhsT_scale=w_scales[:, lo : lo + P],
                         rhs=a_codes[:, g * N : (g + 1) * N].bitcast(FP8X4),
                         rhs_scale=a_scales[:, g * N : (g + 1) * N],
-                        start=first,
-                        stop=last,
+                        start=p == 0,
+                        stop=p == PASSES - 1,
                     )
 
-        for t in range(n_ch + LAG2):
-            u = t - LAG1
-            v = t - LAG2
-            if t < n_ch:
+        for t in range(CHUNKS + 2):
+            u = t - 1
+            v = t - 2
+            if t < CHUNKS:
+                x_to_psum(t)
                 leaky(t)
+                w_gp(t)
                 a_gp(t)
-            if 0 <= u < n_ch:
+            if 0 <= u < CHUNKS:
                 w_scale(u)
                 w_fused(u)
                 a_copy(u)
                 w_copy(u)
-            if 0 <= v < n_ch:
+            if 0 <= v < CHUNKS:
                 quant(v, "a")
                 quant(v, "w")
                 mm(v)

@@ -30,25 +30,30 @@ I_A = 4
 I_WS = 4
 I_WV = 4
 HEAD = 2
-GA = 160
 
 
 BIG = 4
-TWO_FUSED = (8,)
-LEAK_PARTS = [2, 1]
+SHARE = 0
 
 
 def w_engine(i, g):
     if SIZES[i] == BIG:
         if g == 0:
             return "G"
-        return "V" if g == 3 or (g == 2 and i in TWO_FUSED) else "S"
+        return "V" if g == 3 or (g == 2 and i == 8) else "S"
     p = STARTS[i] + g
-    return "V" if p in (1, 3) or p >= 29 else "S"
+    return "V" if p in (1, 3, 29, 30, 31) else "S"
 
 
-def gp_passes(i):
-    return 1 if SIZES[i] == 2 else 0
+def v_share(i, g):
+    return SHARE if SIZES[i] == BIG and g == 1 else 0
+
+
+GP_A = {2: 160, 28: 160}
+
+
+def gp_neurons(i, g):
+    return GP_A.get(STARTS[i] + g, 0)
 
 
 def tile_mnelayer_pb_t_kernel(tc, potential, contribution, out):
@@ -125,31 +130,21 @@ def tile_mnelayer_pb_t_kernel(tc, potential, contribution, out):
             elif sz < BIG:
                 part(0, sz * width, flat[:, 0 : sz * width])
             else:
-                lo = 0
-                for w in LEAK_PARTS:
-                    part(lo * width, (lo + w) * width, flat[:, lo * width : (lo + w) * width])
-                    lo += w
-                for h in range(2):
-                    at = 3 * width + h * BANK
-                    part(at, at + BANK, st[("copy", i)][h][:])
+                part(0, 3 * width, flat[:, 0 : 3 * width])
+                st[("rest", i)] = lambda: part(3 * width, 4 * width, st[("copy", i)][:])
             st[("leak", i)] = leak
             st[("a_grp", i)] = work.tile([P, MAX, N, PACK], BF16, name="a_grp", tag="a_grp", align_bytes=64)
             st[("w_grp", i)] = work.tile([P, MAX, N, PACK], BF16, name="w_grp", tag="w_grp", align_bytes=64)
 
         def x_to_psum(i):
             if SIZES[i] == BIG:
-                halves = []
+                copy = copies.tile([P, PACK * N], BF16, name="copy", tag="copy")
                 for h in range(2):
-                    half = copies.tile([P, BANK], F32, name="half%d" % h, tag="half%d" % h)
+                    cols = slice(h * BANK, (h + 1) * BANK)
                     nc.tensor.matmul(
-                        out=half[:],
-                        lhsT=ident[:],
-                        rhs=raws[i][:, 3, h * BANK : (h + 1) * BANK],
-                        start=True,
-                        stop=True,
+                        out=copy[:, cols], lhsT=ident[:], rhs=raws[i][:, 3, cols], start=True, stop=True
                     )
-                    halves.append(half)
-                st[("copy", i)] = halves
+                st[("copy", i)] = copy
 
         def w_gp(i):
             for g in range(SIZES[i]):
@@ -163,20 +158,21 @@ def tile_mnelayer_pb_t_kernel(tc, potential, contribution, out):
                     )
 
         def a_gp(i):
-            k = gp_passes(i)
-            if k > 0:
-                nc.gpsimd.tensor_scalar(
-                    out=st[("a_grp", i)][:, 0:k, 0:GA, :],
-                    in0=st[("leak", i)][:, 0:k, :, 0:GA].rearrange("p g t n -> p g n t"),
-                    scalar1=1.0,
-                    scalar2=0.0,
-                    op0=ALU.mult,
-                    op1=ALU.add,
-                )
+            for g in range(SIZES[i]):
+                hi = gp_neurons(i, g)
+                if hi > 0:
+                    nc.gpsimd.tensor_scalar(
+                        out=st[("a_grp", i)][:, g, 0:hi, :],
+                        in0=st[("leak", i)][:, g, :, 0:hi].rearrange("p t n -> p n t"),
+                        scalar1=1.0,
+                        scalar2=0.0,
+                        op0=ALU.mult,
+                        op1=ALU.add,
+                    )
 
         def a_copy(i):
             for g in range(SIZES[i]):
-                lo = GA if g < gp_passes(i) else 0
+                lo = gp_neurons(i, g)
                 nc.scalar.copy(
                     out=grp(st[("a_grp", i)][:, g, lo:N, :], I_A),
                     in_=nat(st[("leak", i)][:, g, :, lo:N], I_A),
@@ -186,11 +182,12 @@ def tile_mnelayer_pb_t_kernel(tc, potential, contribution, out):
             for g in range(SIZES[i]):
                 if w_engine(i, g) == "S":
                     p = STARTS[i] + g
+                    lo = v_share(i, g)
                     w_nat = nats.tile([P, PACK, N], BF16, name="w_nat", tag="w_nat")
                     for j in range(PACK):
                         nc.scalar.activation(
-                            out=w_nat[:, j, :],
-                            in_=st[("leak", i)][:, g, j, :],
+                            out=w_nat[:, j, lo:N],
+                            in_=st[("leak", i)][:, g, j, lo:N],
                             func=ACTF.Copy,
                             scale=c32[:, p * PACK + j : p * PACK + j + 1],
                         )
@@ -199,16 +196,21 @@ def tile_mnelayer_pb_t_kernel(tc, potential, contribution, out):
         def w_copy(i):
             for g in range(SIZES[i]):
                 if w_engine(i, g) == "S":
-                    nc.scalar.copy(out=grp(st[("w_grp", i)][:, g], I_WS), in_=nat(st[("w_nat", i, g)][:], I_WS))
+                    lo = v_share(i, g)
+                    nc.scalar.copy(
+                        out=grp(st[("w_grp", i)][:, g, lo:N, :], I_WS),
+                        in_=nat(st[("w_nat", i, g)][:, :, lo:N], I_WS),
+                    )
 
         def w_fused(i):
             for g in range(SIZES[i]):
-                if w_engine(i, g) == "V":
+                hi = N if w_engine(i, g) == "V" else v_share(i, g)
+                if hi > 0:
                     p = STARTS[i] + g
                     nc.vector.tensor_tensor(
-                        out=grp(st[("w_grp", i)][:, g], I_WV),
-                        in0=nat(st[("leak", i)][:, g], I_WV),
-                        in1=nat(c_ps[:, :, p : p + 1].to_broadcast([P, PACK, N]), I_WV),
+                        out=grp(st[("w_grp", i)][:, g, 0:hi, :], I_WV),
+                        in0=nat(st[("leak", i)][:, g, :, 0:hi], I_WV),
+                        in1=nat(c_ps[:, :, p : p + 1].to_broadcast([P, PACK, hi]), I_WV),
                         op=ALU.mult,
                     )
 
@@ -247,6 +249,11 @@ def tile_mnelayer_pb_t_kernel(tc, potential, contribution, out):
             if t < CHUNKS:
                 x_to_psum(t)
                 leaky(t)
+            if 0 <= v < CHUNKS:
+                quant(v, "a")
+            if t < CHUNKS:
+                if SIZES[t] == BIG:
+                    st[("rest", t)]()
                 w_gp(t)
                 a_gp(t)
             if 0 <= u < CHUNKS:
@@ -255,7 +262,6 @@ def tile_mnelayer_pb_t_kernel(tc, potential, contribution, out):
                 a_copy(u)
                 w_copy(u)
             if 0 <= v < CHUNKS:
-                quant(v, "a")
                 quant(v, "w")
                 mm(v)
 

@@ -33,23 +33,20 @@ HEAD = 2
 
 
 BIG = 4
-SHARE = 0
+TWO_FUSED = (4,)
+LAG = 3
 
 
 def w_engine(i, g):
     if SIZES[i] == BIG:
         if g == 0:
             return "G"
-        return "V" if g == 3 or (g == 2 and i == 8) else "S"
+        return "V" if g == 3 or (g == 2 and i in TWO_FUSED) else "S"
     p = STARTS[i] + g
-    return "V" if p in (1, 3, 29, 30, 31) else "S"
+    return "V" if p in (1, 3, 29, 30) else "S"
 
 
-def v_share(i, g):
-    return SHARE if SIZES[i] == BIG and g == 1 else 0
-
-
-GP_A = {2: 160, 28: 160}
+GP_A = {2: 160, 28: 160, 30: 128, 31: 128}
 
 
 def gp_neurons(i, g):
@@ -62,7 +59,8 @@ def tile_mnelayer_pb_t_kernel(tc, potential, contribution, out):
     with ExitStack() as ctx:
         keep = ctx.enter_context(tc.tile_pool(name="keep", bufs=1))
         work = ctx.enter_context(tc.tile_pool(name="work", bufs=BUFS))
-        nats = ctx.enter_context(tc.tile_pool(name="nats", bufs=6))
+        grps = ctx.enter_context(tc.tile_pool(name="grps", bufs=BUFS + 1))
+        nats = ctx.enter_context(tc.tile_pool(name="nats", bufs=4))
         copies = ctx.enter_context(tc.psum_pool(name="copies", bufs=2))
         psum = ctx.enter_context(tc.psum_pool(name="psum", bufs=1))
         ctx.enter_context(tc.manual_schedule())
@@ -131,20 +129,28 @@ def tile_mnelayer_pb_t_kernel(tc, potential, contribution, out):
                 part(0, sz * width, flat[:, 0 : sz * width])
             else:
                 part(0, 3 * width, flat[:, 0 : 3 * width])
-                st[("rest", i)] = lambda: part(3 * width, 4 * width, st[("copy", i)][:])
+                st[("rest", i)] = [
+                    (3 * width + h * BANK, 3 * width + (h + 1) * BANK, st[("copy", i)][h][:]) for h in range(2)
+                ]
+                st[("part", i)] = part
             st[("leak", i)] = leak
-            st[("a_grp", i)] = work.tile([P, MAX, N, PACK], BF16, name="a_grp", tag="a_grp", align_bytes=64)
-            st[("w_grp", i)] = work.tile([P, MAX, N, PACK], BF16, name="w_grp", tag="w_grp", align_bytes=64)
+            st[("a_grp", i)] = grps.tile([P, MAX, N, PACK], BF16, name="a_grp", tag="a_grp", align_bytes=64)
+            st[("w_grp", i)] = grps.tile([P, MAX, N, PACK], BF16, name="w_grp", tag="w_grp", align_bytes=64)
 
         def x_to_psum(i):
             if SIZES[i] == BIG:
-                copy = copies.tile([P, PACK * N], BF16, name="copy", tag="copy")
+                halves = []
                 for h in range(2):
-                    cols = slice(h * BANK, (h + 1) * BANK)
+                    half = copies.tile([P, BANK], F32, name="half%d" % h, tag="half%d" % h)
                     nc.tensor.matmul(
-                        out=copy[:, cols], lhsT=ident[:], rhs=raws[i][:, 3, cols], start=True, stop=True
+                        out=half[:],
+                        lhsT=ident[:],
+                        rhs=raws[i][:, 3, h * BANK : (h + 1) * BANK],
+                        start=True,
+                        stop=True,
                     )
-                st[("copy", i)] = copy
+                    halves.append(half)
+                st[("copy", i)] = halves
 
         def w_gp(i):
             for g in range(SIZES[i]):
@@ -182,12 +188,11 @@ def tile_mnelayer_pb_t_kernel(tc, potential, contribution, out):
             for g in range(SIZES[i]):
                 if w_engine(i, g) == "S":
                     p = STARTS[i] + g
-                    lo = v_share(i, g)
                     w_nat = nats.tile([P, PACK, N], BF16, name="w_nat", tag="w_nat")
                     for j in range(PACK):
                         nc.scalar.activation(
-                            out=w_nat[:, j, lo:N],
-                            in_=st[("leak", i)][:, g, j, lo:N],
+                            out=w_nat[:, j, :],
+                            in_=st[("leak", i)][:, g, j, :],
                             func=ACTF.Copy,
                             scale=c32[:, p * PACK + j : p * PACK + j + 1],
                         )
@@ -196,21 +201,19 @@ def tile_mnelayer_pb_t_kernel(tc, potential, contribution, out):
         def w_copy(i):
             for g in range(SIZES[i]):
                 if w_engine(i, g) == "S":
-                    lo = v_share(i, g)
                     nc.scalar.copy(
-                        out=grp(st[("w_grp", i)][:, g, lo:N, :], I_WS),
-                        in_=nat(st[("w_nat", i, g)][:, :, lo:N], I_WS),
+                        out=grp(st[("w_grp", i)][:, g], I_WS),
+                        in_=nat(st[("w_nat", i, g)][:], I_WS),
                     )
 
         def w_fused(i):
             for g in range(SIZES[i]):
-                hi = N if w_engine(i, g) == "V" else v_share(i, g)
-                if hi > 0:
+                if w_engine(i, g) == "V":
                     p = STARTS[i] + g
                     nc.vector.tensor_tensor(
-                        out=grp(st[("w_grp", i)][:, g, 0:hi, :], I_WV),
-                        in0=nat(st[("leak", i)][:, g, :, 0:hi], I_WV),
-                        in1=nat(c_ps[:, :, p : p + 1].to_broadcast([P, PACK, hi]), I_WV),
+                        out=grp(st[("w_grp", i)][:, g], I_WV),
+                        in0=nat(st[("leak", i)][:, g], I_WV),
+                        in1=nat(c_ps[:, :, p : p + 1].to_broadcast([P, PACK, N]), I_WV),
                         op=ALU.mult,
                     )
 
@@ -243,9 +246,9 @@ def tile_mnelayer_pb_t_kernel(tc, potential, contribution, out):
                         stop=p == PASSES - 1,
                     )
 
-        for t in range(CHUNKS + 2):
+        for t in range(CHUNKS + LAG):
             u = t - 1
-            v = t - 2
+            v = t - LAG
             if t < CHUNKS:
                 x_to_psum(t)
                 leaky(t)
@@ -253,7 +256,8 @@ def tile_mnelayer_pb_t_kernel(tc, potential, contribution, out):
                 quant(v, "a")
             if t < CHUNKS:
                 if SIZES[t] == BIG:
-                    st[("rest", t)]()
+                    for lo, hi, again in st[("rest", t)]:
+                        st[("part", t)](lo, hi, again)
                 w_gp(t)
                 a_gp(t)
             if 0 <= u < CHUNKS:

@@ -128,11 +128,11 @@ def tile_mnelayer_pb_t_kernel(tc, potential, contribution, out):
             elif sz < BIG:
                 part(0, sz * width, flat[:, 0 : sz * width])
             else:
-                part(0, 3 * width, flat[:, 0 : 3 * width])
-                st[("rest", i)] = [
-                    (3 * width + h * BANK, 3 * width + (h + 1) * BANK, st[("copy", i)][h][:]) for h in range(2)
-                ]
-                st[("part", i)] = part
+                part(0, 2 * width, flat[:, 0 : 2 * width])
+                part(2 * width, 3 * width, flat[:, 2 * width : 3 * width])
+                for h in range(2):
+                    at = 3 * width + h * BANK
+                    part(at, at + BANK, st[("copy", i)][h][:])
             st[("leak", i)] = leak
             st[("a_grp", i)] = grps.tile([P, MAX, N, PACK], BF16, name="a_grp", tag="a_grp", align_bytes=64)
             st[("w_grp", i)] = grps.tile([P, MAX, N, PACK], BF16, name="w_grp", tag="w_grp", align_bytes=64)
@@ -252,12 +252,7 @@ def tile_mnelayer_pb_t_kernel(tc, potential, contribution, out):
             if t < CHUNKS:
                 x_to_psum(t)
                 leaky(t)
-            if 0 <= v < CHUNKS:
-                quant(v, "a")
             if t < CHUNKS:
-                if SIZES[t] == BIG:
-                    for lo, hi, again in st[("rest", t)]:
-                        st[("part", t)](lo, hi, again)
                 w_gp(t)
                 a_gp(t)
             if 0 <= u < CHUNKS:
@@ -266,6 +261,7 @@ def tile_mnelayer_pb_t_kernel(tc, potential, contribution, out):
                 a_copy(u)
                 w_copy(u)
             if 0 <= v < CHUNKS:
+                quant(v, "a")
                 quant(v, "w")
                 mm(v)
 

@@ -26,9 +26,9 @@ STARTS = [sum(SIZES[:i]) for i in range(len(SIZES))]
 CHUNKS = len(SIZES)
 MAX = max(SIZES)
 BUFS = 3
-I_A = 4
-I_WS = 4
-I_WV = 4
+I_A = 2
+I_WS = 2
+I_WV = 2
 HEAD = 2
 
 

from contextlib import ExitStack

import concourse.mybir as mybir
from concourse.masks import make_identity

FLOPS = 2 * 16384 * 256 * 256

BF16 = mybir.dt.bfloat16
F32 = mybir.dt.float32
U32 = mybir.dt.uint32
U8 = mybir.dt.uint8
FP8X4 = mybir.dt.float8_e4m3fn_x4
ALU = mybir.AluOpType
ACTF = mybir.ActivationFunctionType

P = 128
PACK = 4
N = 256
B = 16384
K_PASS = P * PACK
BANK = 512
PASSES = B // K_PASS
SLOPE = 0.01
SIZES = [1, 1, 2] + [4] * 6 + [2, 1, 1]
STARTS = [sum(SIZES[:i]) for i in range(len(SIZES))]
CHUNKS = len(SIZES)
MAX = max(SIZES)
BUFS = 3
I_A = 2
I_WS = 2
I_WV = 2
HEAD = 2


BIG = 4
TWO_FUSED = (4,)
LAG = 3


def w_engine(i, g):
    if SIZES[i] == BIG:
        if g == 0:
            return "G"
        return "V" if g == 3 or (g == 2 and i in TWO_FUSED) else "S"
    p = STARTS[i] + g
    return "V" if p in (1, 3, 29, 30) else "S"


GP_A = {2: 160, 28: 160, 30: 128, 31: 128}


def gp_neurons(i, g):
    return GP_A.get(STARTS[i] + g, 0)


def tile_mnelayer_pb_t_kernel(tc, potential, contribution, out):
    nc = tc.nc
    assert sum(SIZES) == PASSES and SIZES[0] == 1
    with ExitStack() as ctx:
        keep = ctx.enter_context(tc.tile_pool(name="keep", bufs=1))
        work = ctx.enter_context(tc.tile_pool(name="work", bufs=BUFS))
        grps = ctx.enter_context(tc.tile_pool(name="grps", bufs=BUFS + 1))
        nats = ctx.enter_context(tc.tile_pool(name="nats", bufs=4))
        copies = ctx.enter_context(tc.psum_pool(name="copies", bufs=2))
        psum = ctx.enter_context(tc.psum_pool(name="psum", bufs=1))
        ctx.enter_context(tc.manual_schedule())

        pot = potential.rearrange("(g p j) n -> p g (j n)", p=P, j=PACK)

        raws = []
        for i in range(CHUNKS):
            raw = keep.tile([P, SIZES[i], PACK * N], BF16, name="raw%d" % i)
            raws.append(raw)
        head = PACK * N // HEAD
        for h in range(HEAD):
            cols = slice(h * head, (h + 1) * head)
            nc.sync.dma_start(out=raws[0][:, :, cols], in_=pot[:, 0:1, cols])
        for i in range(1, CHUNKS):
            nc.sync.dma_start(out=raws[i][:], in_=pot[:, STARTS[i] : STARTS[i] + SIZES[i], :])

        c_rows = keep.tile([P, K_PASS], BF16)
        nc.vector.memset(c_rows[32:64, :], 0.0)
        nc.vector.memset(c_rows[64:128, :], 0.0)
        nc.scalar.dma_start(out=c_rows[0:PASSES, :], in_=contribution.rearrange("(g k) -> g k", k=K_PASS))
        ident = keep.tile([P, P], BF16)
        make_identity(nc, ident[:])
        c_ps = psum.tile([P, PACK, P], BF16)
        c32 = keep.tile([P, PASSES * PACK], F32)
        for j in range(PACK):
            nc.tensor.transpose(c_ps[:, j, :], c_rows[:, j : K_PASS : PACK], ident[:])
        nc.scalar.activation(
            out=c32[:].rearrange("p (g j) -> p g j", j=PACK),
            in_=c_ps[:, :, 0:PASSES].rearrange("p j g -> p g j"),
            func=ACTF.Copy,
        )

        acc0 = psum.tile([P, N], F32)
        acc1 = psum.tile([P, N], F32)
        accs = [acc0, acc1]
        st = {}

        def grp(dst, i):
            return dst.rearrange("p (c i) t -> p c t i", i=i)

        def nat(src, i):
            return src.rearrange("p t (c i) -> p c t i", i=i)

        def leaky(i):
            sz = SIZES[i]
            leak = work.tile([P, MAX, PACK, N], F32, name="leak", tag="leak")
            flat = raws[i][:].rearrange("p g f -> p (g f)")
            flat_out = leak[:, 0:sz].rearrange("p g j n -> p (g j n)")

            def part(lo, hi, again):
                nc.vector.scalar_tensor_tensor(
                    out=flat_out[:, lo:hi],
                    in0=flat[:, lo:hi],
                    scalar=SLOPE,
                    in1=again,
                    op0=ALU.mult,
                    op1=ALU.max,
                )

            width = PACK * N
            if i == 0:
                for h in range(HEAD):
                    part(h * head, (h + 1) * head, flat[:, h * head : (h + 1) * head])
            elif sz < BIG:
                part(0, sz * width, flat[:, 0 : sz * width])
            else:
                part(0, 2 * width, flat[:, 0 : 2 * width])
                part(2 * width, 3 * width, flat[:, 2 * width : 3 * width])
                for h in range(2):
                    at = 3 * width + h * BANK
                    part(at, at + BANK, st[("copy", i)][h][:])
            st[("leak", i)] = leak
            st[("a_grp", i)] = grps.tile([P, MAX, N, PACK], BF16, name="a_grp", tag="a_grp", align_bytes=64)
            st[("w_grp", i)] = grps.tile([P, MAX, N, PACK], BF16, name="w_grp", tag="w_grp", align_bytes=64)

        def x_to_psum(i):
            if SIZES[i] == BIG:
                halves = []
                for h in range(2):
                    half = copies.tile([P, BANK], F32, name="half%d" % h, tag="half%d" % h)
                    nc.tensor.matmul(
                        out=half[:],
                        lhsT=ident[:],
                        rhs=raws[i][:, 3, h * BANK : (h + 1) * BANK],
                        start=True,
                        stop=True,
                    )
                    halves.append(half)
                st[("copy", i)] = halves

        def w_gp(i):
            for g in range(SIZES[i]):
                if w_engine(i, g) == "G":
                    p = STARTS[i] + g
                    nc.gpsimd.tensor_tensor(
                        out=st[("w_grp", i)][:, g],
                        in0=st[("leak", i)][:, g].rearrange("p t n -> p n t"),
                        in1=c32[:, p * PACK : (p + 1) * PACK].unsqueeze(1).to_broadcast([P, N, PACK]),
                        op=ALU.mult,
                    )

        def a_gp(i):
            for g in range(SIZES[i]):
                hi = gp_neurons(i, g)
                if hi > 0:
                    nc.gpsimd.tensor_scalar(
                        out=st[("a_grp", i)][:, g, 0:hi, :],
                        in0=st[("leak", i)][:, g, :, 0:hi].rearrange("p t n -> p n t"),
                        scalar1=1.0,
                        scalar2=0.0,
                        op0=ALU.mult,
                        op1=ALU.add,
                    )

        def a_copy(i):
            for g in range(SIZES[i]):
                lo = gp_neurons(i, g)
                nc.scalar.copy(
                    out=grp(st[("a_grp", i)][:, g, lo:N, :], I_A),
                    in_=nat(st[("leak", i)][:, g, :, lo:N], I_A),
                )

        def w_scale(i):
            for g in range(SIZES[i]):
                if w_engine(i, g) == "S":
                    p = STARTS[i] + g
                    w_nat = nats.tile([P, PACK, N], BF16, name="w_nat", tag="w_nat")
                    for j in range(PACK):
                        nc.scalar.activation(
                            out=w_nat[:, j, :],
                            in_=st[("leak", i)][:, g, j, :],
                            func=ACTF.Copy,
                            scale=c32[:, p * PACK + j : p * PACK + j + 1],
                        )
                    st[("w_nat", i, g)] = w_nat

        def w_copy(i):
            for g in range(SIZES[i]):
                if w_engine(i, g) == "S":
                    nc.scalar.copy(
                        out=grp(st[("w_grp", i)][:, g], I_WS),
                        in_=nat(st[("w_nat", i, g)][:], I_WS),
                    )

        def w_fused(i):
            for g in range(SIZES[i]):
                if w_engine(i, g) == "V":
                    p = STARTS[i] + g
                    nc.vector.tensor_tensor(
                        out=grp(st[("w_grp", i)][:, g], I_WV),
                        in0=nat(st[("leak", i)][:, g], I_WV),
                        in1=nat(c_ps[:, :, p : p + 1].to_broadcast([P, PACK, N]), I_WV),
                        op=ALU.mult,
                    )

        def quant(i, what):
            sz = SIZES[i]
            g4 = st[(what + "_grp", i)]
            codes = work.tile([P, MAX * N], U32, name=what + "_codes", tag=what + "_codes", align_bytes=64)
            scales = work.tile([P, MAX * N], U8, name=what + "_scales", tag=what + "_scales", align_bytes=64)
            nc.vector.quantize_mx(
                out=codes[:, 0 : sz * N].bitcast(FP8X4),
                scales=scales[:, 0 : sz * N],
                in_=g4[:, 0:sz].rearrange("p g n t -> p (g n t)"),
            )
            st[(what + "_q", i)] = (codes, scales)

        def mm(i):
            a_codes, a_scales = st[("a_q", i)]
            w_codes, w_scales = st[("w_q", i)]
            for g in range(SIZES[i]):
                p = STARTS[i] + g
                for m in range(2):
                    lo = g * N + m * P
                    nc.tensor.matmul_mx(
                        out=accs[m][:],
                        lhsT=w_codes[:, lo : lo + P].bitcast(FP8X4),
                        lhsT_scale=w_scales[:, lo : lo + P],
                        rhs=a_codes[:, g * N : (g + 1) * N].bitcast(FP8X4),
                        rhs_scale=a_scales[:, g * N : (g + 1) * N],
                        start=p == 0,
                        stop=p == PASSES - 1,
                    )

        for t in range(CHUNKS + LAG):
            u = t - 1
            v = t - LAG
            if t < CHUNKS:
                x_to_psum(t)
                leaky(t)
            if t < CHUNKS:
                w_gp(t)
                a_gp(t)
            if 0 <= u < CHUNKS:
                w_scale(u)
                w_fused(u)
                a_copy(u)
                w_copy(u)
            if 0 <= v < CHUNKS:
                quant(v, "a")
                quant(v, "w")
                mm(v)

        res0 = keep.tile([P, N], F32)
        res1 = keep.tile([P, N], F32)
        nc.vector.tensor_scalar(
            out=res0[:], in0=acc0[:], scalar1=1.0 / B, scalar2=None, op0=ALU.mult
        )
        nc.scalar.activation(out=res1[:], in_=acc1[:], func=ACTF.Copy, scale=1.0 / B)
        nc.sync.dma_start(out=out[0:P, :], in_=res0[:])
        nc.sync.dma_start(out=out[P : 2 * P, :], in_=res1[:])
